import numpy as np
import ml_dtypes


def mxq(x, axis, fmt="e4m3"):
    dtype, down = {"e4m3": (ml_dtypes.float8_e4m3fn, 7), "e5m2": (ml_dtypes.float8_e5m2, 14)}[fmt]
    v = np.moveaxis(np.asarray(x, np.float32).astype(ml_dtypes.bfloat16).astype(np.float64), axis, -1)
    blocks = v.reshape(v.shape[:-1] + (-1, 32))
    amax = np.abs(blocks).max(-1, keepdims=True)
    byte = np.maximum(np.where(amax > 0, np.frexp(amax)[1] - 1 + 127, 0) - down, 1)
    scale = np.exp2(byte - 127.0)
    codes = (blocks / scale).astype(np.float32).astype(dtype).astype(np.float64)
    return np.moveaxis((codes * scale).reshape(v.shape), -1, axis)


BF16 = ml_dtypes.bfloat16


def bf(x):
    return np.asarray(x, np.float32).astype(BF16)


def f64(x):
    return np.asarray(x).astype(np.float64)


B, C, H, W, O, K, S, P = 2, 256, 31, 31, 128, 2, 1, 1
KD = C * K * K


def unfold(x, k, s, p):
    b, c, h, w = x.shape
    ho = (h + 2 * p - k) // s + 1
    wo = (w + 2 * p - k) // s + 1
    xp = np.pad(x, ((0, 0), (0, 0), (p, p), (p, p)))
    pats = np.stack([xp[:, :, i:i + s * ho:s, j:j + s * wo:s] for i in range(k) for j in range(k)], axis=2)
    return pats.reshape(b, c * k * k, ho * wo), ho, wo


def setup_inputs():
    mu = np.random.standard_normal(C)
    g = np.random.standard_normal(O)
    x = (mu[None, :, None, None] + np.random.standard_normal((B, C, H, W))) / np.sqrt(KD)
    weight = (g[:, None] * np.repeat(mu, K * K)[None, :] + np.random.standard_normal((O, KD))) / np.sqrt(KD)
    return {"x": bf(x), "weight": bf(weight)}


def reference(x, weight):
    x, weight = f64(x), f64(weight)
    pats, ho, wo = unfold(x, K, S, P)
    x2 = np.sum(pats * pats, axis=1)
    w2 = np.sum(weight * weight, axis=1)
    pt = pats.reshape(B, C, K * K, ho * wo).transpose(0, 2, 1, 3).reshape(B, KD, ho * wo)
    wt = weight.reshape(O, C, K * K).transpose(0, 2, 1).reshape(O, KD)
    xw = mxq(wt, 1, "e4m3") @ mxq(pt, 1, "e4m3")
    d2 = np.maximum(x2[:, None, :] + w2[None, :, None] - 2.0 * xw, 0.0)
    return d2.reshape(B, O, ho, wo)

@@ -1,0 +1,195 @@
+import concourse.mybir as mybir
+from concourse.masks import make_identity
+
+F32 = mybir.dt.float32
+BF16 = mybir.dt.bfloat16
+I32 = mybir.dt.int32
+U32 = mybir.dt.uint32
+U8 = mybir.dt.uint8
+FP8X4 = mybir.dt.float8_e4m3fn_x4
+ACT = mybir.ActivationFunctionType
+ALU = mybir.AluOpType
+
+P = 128
+PACK = 4
+B = 2
+SIDE = 31
+OUT = 32
+PAD_ROWS = OUT + 1
+ROW = B * OUT
+CHUNK = 128
+ROUND_ROWS = 8
+ROUND_COLS = ROUND_ROWS * ROW
+ROUND_CHUNKS = ROUND_COLS // CHUNK
+ROUNDS = OUT // ROUND_ROWS
+CHUNKS = ROUNDS * ROUND_CHUNKS
+COLS = PAD_ROWS * ROW
+
+FLOPS = 2 * B * OUT * OUT * P * 1024
+
+
+def tile_rbf_conv2d_s_kernel(tc, x, weight, out):
+    nc = tc.nc
+    with (
+        tc.tile_pool(name="keep", bufs=1) as keep,
+        tc.tile_pool(name="work", bufs=2) as work,
+        tc.psum_pool(name="psum_w", bufs=1) as psum_w,
+        tc.psum_pool(name="psum", bufs=2) as psum,
+    ):
+        w_sb = keep.tile([P, 1024], BF16)
+        nc.scalar.dma_start(out=w_sb[:], in_=weight)
+        raw = []
+        for b in range(B):
+            raw_b = keep.tile([P, 2, SIDE, SIDE], BF16, name="raw%d" % b)
+            nc.sync.dma_start(
+                out=raw_b[:].rearrange("p e y z -> p (e y z)"),
+                in_=x[b].rearrange("(p e) y z -> p (e y z)", e=2),
+            )
+            raw.append(raw_b)
+
+        ident_bf = keep.tile([P, P], BF16)
+        make_identity(nc, ident_bf[:])
+        wide = keep.tile([P, 3 * P], F32)
+        nc.gpsimd.memset(wide[:], 0.0)
+        make_identity(nc, wide[:, P : 2 * P], nomemset=True)
+        ident = wide[:, P : 2 * P]
+        pairs = keep.tile([P, 2 * P + ROW], F32)
+        nc.vector.tensor_tensor(
+            out=pairs[:], in0=wide[:, 0 : 2 * P + ROW], in1=wide[:, 1 : 2 * P + ROW + 1], op=ALU.add
+        )
+        taps = keep.tile([P, 2 * P], F32)
+        nc.vector.tensor_tensor(
+            out=taps[:], in0=pairs[:, 0 : 2 * P], in1=pairs[:, ROW : 2 * P + ROW], op=ALU.add
+        )
+        taps_next = taps[:, 0:P]
+        taps_same = taps[:, P : 2 * P]
+
+        grouped = keep.tile([P, COLS * PACK], BF16, align_bytes=64)
+        nc.vector.memset(grouped[:].bitcast(I32), 0)
+        grouped_v = grouped[:].rearrange(
+            "p (y b z k e) -> p y b z k e", y=PAD_ROWS, b=B, z=OUT, k=2, e=2
+        )
+        grouped_w = grouped[:].bitcast(F32).rearrange("p (c k) -> p c k", k=2)
+        x_codes = keep.tile([P, COLS], U32, align_bytes=64)
+        x_scales = keep.tile([P, COLS], U8, align_bytes=64)
+
+        w2 = keep.tile([P, 1], F32)
+        w_squares = keep.tile([P, 1024], BF16)
+        nc.scalar.activation(out=w_squares[:], in_=w_sb[:], func=ACT.Square, accum_out=w2[:])
+        w_by_k = w_sb[:].rearrange("o (u k) -> o k u", k=8)
+        w_t = psum_w.tile([P, 8, P], BF16)
+        for kh in range(2):
+            for kw in range(2):
+                for e in range(2):
+                    nc.tensor.transpose(
+                        w_t[:, 4 * kh + 2 * kw + e, :], w_by_k[:, 4 * e + 2 * kh + kw, :], ident_bf[:]
+                    )
+        w_grouped = keep.tile([P, 2, P, PACK], BF16, align_bytes=64)
+        nc.scalar.copy(
+            out=w_grouped[:], in_=w_t[:].rearrange("u (h t) o -> u h o t", h=2)
+        )
+        w_codes = keep.tile([P, 2 * P], U32, align_bytes=64)
+        w_scales = keep.tile([P, 2 * P], U8, align_bytes=64)
+        nc.vector.quantize_mx(
+            out=w_codes[:].bitcast(FP8X4),
+            scales=w_scales[:],
+            in_=w_grouped[:].rearrange("u h o t -> u (h o t)"),
+        )
+
+        pixel_sq = keep.tile([P, CHUNKS + 1], F32)
+        nc.vector.memset(pixel_sq[:], 0.0)
+        squares = keep.tile([P, CHUNKS, 2 * P], BF16)
+        x2_sb = keep.tile([P, CHUNKS], F32)
+
+        def prepare(r):
+            first = max(ROUND_ROWS * r, 1)
+            last = ROUND_ROWS * (r + 1)
+            for b in range(B):
+                for kw in range(2):
+                    nc.vector.tensor_copy(
+                        out=grouped_v[:, first:last, b, 1 - kw : 1 - kw + SIDE, kw, :],
+                        in_=raw[b][:, :, first - 1 : last - 1, :].rearrange("p e y z -> p y z e"),
+                    )
+            cols = slice(ROUND_COLS * r, ROUND_COLS * (r + 1))
+            nc.vector.quantize_mx(
+                out=x_codes[:, cols].bitcast(FP8X4),
+                scales=x_scales[:, cols],
+                in_=grouped[:, PACK * ROUND_COLS * r : PACK * ROUND_COLS * (r + 1)],
+            )
+            x_t = psum.tile([P, ROUND_CHUNKS, P], F32)
+            for c in range(ROUND_CHUNKS):
+                chunk = ROUND_CHUNKS * r + c
+                nc.tensor.transpose(
+                    x_t[:, c, :], grouped_w[:, CHUNK * chunk : CHUNK * (chunk + 1), 0], ident
+                )
+            for c in range(ROUND_CHUNKS):
+                chunk = ROUND_CHUNKS * r + c
+                nc.scalar.activation(
+                    out=squares[:, chunk, :],
+                    in_=x_t[:, c, :].bitcast(BF16),
+                    func=ACT.Square,
+                    accum_out=pixel_sq[:, chunk : chunk + 1],
+                )
+
+        def finish(r):
+            chunks = slice(ROUND_CHUNKS * r, ROUND_CHUNKS * (r + 1))
+            xw = psum.tile([P, ROUND_CHUNKS, P], F32)
+            for c in range(ROUND_CHUNKS):
+                for kh in range(2):
+                    start = CHUNK * (ROUND_CHUNKS * r + c) + ROW * kh
+                    nc.tensor.matmul_mx(
+                        out=xw[:, c, :],
+                        lhsT=x_codes[:, start : start + CHUNK].bitcast(FP8X4),
+                        lhsT_scale=x_scales[:, start : start + CHUNK],
+                        rhs=w_codes[:, P * kh : P * (kh + 1)].bitcast(FP8X4),
+                        rhs_scale=w_scales[:, P * kh : P * (kh + 1)],
+                        start=(kh == 0),
+                        stop=(kh == 1),
+                    )
+            x2_ps = psum_w.tile([P, ROUND_CHUNKS], F32)
+            nc.tensor.matmul(
+                out=x2_ps[:], lhsT=taps_same, rhs=pixel_sq[:, chunks], start=True, stop=False
+            )
+            nc.tensor.matmul(
+                out=x2_ps[:],
+                lhsT=taps_next,
+                rhs=pixel_sq[:, ROUND_CHUNKS * r + 1 : ROUND_CHUNKS * (r + 1) + 1],
+                start=False,
+                stop=True,
+            )
+            nc.vector.tensor_copy(out=x2_sb[:, chunks], in_=x2_ps[:])
+            partial = work.tile([P, ROUND_CHUNKS, P], F32)
+            nc.vector.scalar_tensor_tensor(
+                out=partial[:],
+                in0=xw[:],
+                scalar=-2.0,
+                in1=x2_sb[:, chunks].unsqueeze(2).to_broadcast([P, ROUND_CHUNKS, P]),
+                op0=ALU.mult,
+                op1=ALU.add,
+            )
+            turned = psum.tile([P, ROUND_CHUNKS, P], F32)
+            for c in range(ROUND_CHUNKS):
+                nc.tensor.transpose(turned[:, c, :], partial[:, c, :], ident)
+            result = work.tile([P, B, ROUND_ROWS, OUT], F32)
+            nc.scalar.activation(
+                out=result[:].rearrange("o b y z -> o y b z"),
+                in_=turned[:].rearrange("o c (l b z) -> o (c l) b z", l=2, b=B),
+                func=ACT.Relu,
+                bias=w2[:],
+                scale=1.0,
+            )
+            nc.sync.dma_start(
+                out=out[:, :, ROUND_ROWS * r : ROUND_ROWS * (r + 1), :].rearrange("b o y z -> o b (y z)"),
+                in_=result[:].rearrange("o b y z -> o b (y z)"),
+            )
+
+        for r in range(ROUNDS):
+            prepare(r)
+            if r > 0:
+                finish(r - 1)
+        nc.vector.quantize_mx(
+            out=x_codes[:, ROUNDS * ROUND_COLS : COLS].bitcast(FP8X4),
+            scales=x_scales[:, ROUNDS * ROUND_COLS : COLS],
+            in_=grouped[:, PACK * ROUNDS * ROUND_COLS : PACK * COLS],
+        )
+        finish(ROUNDS - 1)

@@ -28,24 +28,34 @@ COLS = PAD_ROWS * ROW
 FLOPS = 2 * B * OUT * OUT * P * 1024
 
 
+def image_rows(r):
+    return max(ROUND_ROWS * r, 1) - 1, ROUND_ROWS * (r + 1) - 1
+
+
 def tile_rbf_conv2d_s_kernel(tc, x, weight, out):
     nc = tc.nc
     with (
         tc.tile_pool(name="keep", bufs=1) as keep,
-        tc.tile_pool(name="work", bufs=2) as work,
-        tc.psum_pool(name="psum_w", bufs=1) as psum_w,
-        tc.psum_pool(name="psum", bufs=2) as psum,
+        tc.tile_pool(name="work", bufs=ROUNDS) as work,
+        tc.psum_pool(name="psum_small", bufs=1) as psum_small,
+        tc.psum_pool(name="psum_turn", bufs=3) as psum_turn,
+        tc.psum_pool(name="psum_xw", bufs=ROUNDS) as psum_xw,
+        tc.manual_schedule(),
     ):
         w_sb = keep.tile([P, 1024], BF16)
         nc.scalar.dma_start(out=w_sb[:], in_=weight)
         raw = []
-        for b in range(B):
-            raw_b = keep.tile([P, 2, SIDE, SIDE], BF16, name="raw%d" % b)
-            nc.sync.dma_start(
-                out=raw_b[:].rearrange("p e y z -> p (e y z)"),
-                in_=x[b].rearrange("(p e) y z -> p (e y z)", e=2),
-            )
-            raw.append(raw_b)
+        for r in range(ROUNDS):
+            first, last = image_rows(r)
+            raw_r = []
+            for b in range(B):
+                raw_rb = keep.tile([P, 2, last - first, SIDE], BF16, name="raw%d_%d" % (r, b))
+                nc.sync.dma_start(
+                    out=raw_rb[:].rearrange("p e y z -> p e (y z)"),
+                    in_=x[b, :, first:last, :].rearrange("(p e) y z -> p e (y z)", e=2),
+                )
+                raw_r.append(raw_rb)
+            raw.append(raw_r)
 
         ident_bf = keep.tile([P, P], BF16)
         make_identity(nc, ident_bf[:])
@@ -53,19 +63,14 @@ def tile_rbf_conv2d_s_kernel(tc, x, weight, out):
         nc.gpsimd.memset(wide[:], 0.0)
         make_identity(nc, wide[:, P : 2 * P], nomemset=True)
         ident = wide[:, P : 2 * P]
-        pairs = keep.tile([P, 2 * P + ROW], F32)
-        nc.vector.tensor_tensor(
-            out=pairs[:], in0=wide[:, 0 : 2 * P + ROW], in1=wide[:, 1 : 2 * P + ROW + 1], op=ALU.add
-        )
-        taps = keep.tile([P, 2 * P], F32)
-        nc.vector.tensor_tensor(
-            out=taps[:], in0=pairs[:, 0 : 2 * P], in1=pairs[:, ROW : 2 * P + ROW], op=ALU.add
-        )
-        taps_next = taps[:, 0:P]
-        taps_same = taps[:, P : 2 * P]
 
         grouped = keep.tile([P, COLS * PACK], BF16, align_bytes=64)
-        nc.vector.memset(grouped[:].bitcast(I32), 0)
+        grouped_i = grouped[:].bitcast(I32)
+        row_words = 2 * OUT
+        nc.vector.memset(grouped_i[:, 0 : B * row_words], 0)
+        nc.vector.memset(grouped_i[:, 2 * COLS - B * row_words : 2 * COLS], 0)
+        seams = grouped_i[:, row_words - 1 : 2 * COLS - 1].rearrange("p (s w) -> p s w", w=row_words)
+        nc.vector.memset(seams[:, :, 0:2], 0)
         grouped_v = grouped[:].rearrange(
             "p (y b z k e) -> p y b z k e", y=PAD_ROWS, b=B, z=OUT, k=2, e=2
         )
@@ -73,11 +78,27 @@ def tile_rbf_conv2d_s_kernel(tc, x, weight, out):
         x_codes = keep.tile([P, COLS], U32, align_bytes=64)
         x_scales = keep.tile([P, COLS], U8, align_bytes=64)
 
+        pixel_sq = keep.tile([P, CHUNKS + 1], F32)
+        nc.vector.memset(pixel_sq[:], 0.0)
+        squares = keep.tile([P, CHUNKS, 2 * P], BF16)
+        x2_sb = keep.tile([P, CHUNKS], F32)
+
+        pairs = keep.tile([P, 2 * P + ROW], F32)
+        nc.gpsimd.tensor_tensor(
+            out=pairs[:], in0=wide[:, 0 : 2 * P + ROW], in1=wide[:, 1 : 2 * P + ROW + 1], op=ALU.add
+        )
+        taps = keep.tile([P, 2 * P], F32)
+        nc.gpsimd.tensor_tensor(
+            out=taps[:], in0=pairs[:, 0 : 2 * P], in1=pairs[:, ROW : 2 * P + ROW], op=ALU.add
+        )
+        taps_next = taps[:, 0:P]
+        taps_same = taps[:, P : 2 * P]
+
         w2 = keep.tile([P, 1], F32)
         w_squares = keep.tile([P, 1024], BF16)
         nc.scalar.activation(out=w_squares[:], in_=w_sb[:], func=ACT.Square, accum_out=w2[:])
         w_by_k = w_sb[:].rearrange("o (u k) -> o k u", k=8)
-        w_t = psum_w.tile([P, 8, P], BF16)
+        w_t = psum_small.tile([P, 8, P], BF16, tag="small")
         for kh in range(2):
             for kw in range(2):
                 for e in range(2):
@@ -85,38 +106,23 @@ def tile_rbf_conv2d_s_kernel(tc, x, weight, out):
                         w_t[:, 4 * kh + 2 * kw + e, :], w_by_k[:, 4 * e + 2 * kh + kw, :], ident_bf[:]
                     )
         w_grouped = keep.tile([P, 2, P, PACK], BF16, align_bytes=64)
-        nc.scalar.copy(
-            out=w_grouped[:], in_=w_t[:].rearrange("u (h t) o -> u h o t", h=2)
-        )
+        nc.scalar.copy(out=w_grouped[:], in_=w_t[:].rearrange("u (h t) o -> u h o t", h=2))
         w_codes = keep.tile([P, 2 * P], U32, align_bytes=64)
         w_scales = keep.tile([P, 2 * P], U8, align_bytes=64)
-        nc.vector.quantize_mx(
-            out=w_codes[:].bitcast(FP8X4),
-            scales=w_scales[:],
-            in_=w_grouped[:].rearrange("u h o t -> u (h o t)"),
-        )
 
-        pixel_sq = keep.tile([P, CHUNKS + 1], F32)
-        nc.vector.memset(pixel_sq[:], 0.0)
-        squares = keep.tile([P, CHUNKS, 2 * P], BF16)
-        x2_sb = keep.tile([P, CHUNKS], F32)
+        def quantise(codes, scales, values):
+            nc.vector.quantize_mx(out=codes.bitcast(FP8X4), scales=scales, in_=values)
 
-        def prepare(r):
-            first = max(ROUND_ROWS * r, 1)
-            last = ROUND_ROWS * (r + 1)
+        def regroup(r, kw):
+            first, last = image_rows(r)
             for b in range(B):
-                for kw in range(2):
-                    nc.vector.tensor_copy(
-                        out=grouped_v[:, first:last, b, 1 - kw : 1 - kw + SIDE, kw, :],
-                        in_=raw[b][:, :, first - 1 : last - 1, :].rearrange("p e y z -> p y z e"),
-                    )
-            cols = slice(ROUND_COLS * r, ROUND_COLS * (r + 1))
-            nc.vector.quantize_mx(
-                out=x_codes[:, cols].bitcast(FP8X4),
-                scales=x_scales[:, cols],
-                in_=grouped[:, PACK * ROUND_COLS * r : PACK * ROUND_COLS * (r + 1)],
-            )
-            x_t = psum.tile([P, ROUND_CHUNKS, P], F32)
+                nc.vector.tensor_copy(
+                    out=grouped_v[:, first + 1 : last + 1, b, 1 - kw : 1 - kw + SIDE, kw, :],
+                    in_=raw[r][b][:].rearrange("p e y z -> p y z e"),
+                )
+
+        def pixel_sums(r):
+            x_t = psum_turn.tile([P, ROUND_CHUNKS, P], F32, tag="turn")
             for c in range(ROUND_CHUNKS):
                 chunk = ROUND_CHUNKS * r + c
                 nc.tensor.transpose(
@@ -131,9 +137,8 @@ def tile_rbf_conv2d_s_kernel(tc, x, weight, out):
                     accum_out=pixel_sq[:, chunk : chunk + 1],
                 )
 
-        def finish(r):
-            chunks = slice(ROUND_CHUNKS * r, ROUND_CHUNKS * (r + 1))
-            xw = psum.tile([P, ROUND_CHUNKS, P], F32)
+        def multiply(r):
+            xw = psum_xw.tile([P, ROUND_CHUNKS, P], F32)
             for c in range(ROUND_CHUNKS):
                 for kh in range(2):
                     start = CHUNK * (ROUND_CHUNKS * r + c) + ROW * kh
@@ -146,50 +151,78 @@ def tile_rbf_conv2d_s_kernel(tc, x, weight, out):
                         start=(kh == 0),
                         stop=(kh == 1),
                     )
-            x2_ps = psum_w.tile([P, ROUND_CHUNKS], F32)
-            nc.tensor.matmul(
-                out=x2_ps[:], lhsT=taps_same, rhs=pixel_sq[:, chunks], start=True, stop=False
-            )
-            nc.tensor.matmul(
-                out=x2_ps[:],
-                lhsT=taps_next,
-                rhs=pixel_sq[:, ROUND_CHUNKS * r + 1 : ROUND_CHUNKS * (r + 1) + 1],
-                start=False,
-                stop=True,
-            )
-            nc.vector.tensor_copy(out=x2_sb[:, chunks], in_=x2_ps[:])
+            return xw
+
+        def combine(r, xw):
             partial = work.tile([P, ROUND_CHUNKS, P], F32)
             nc.vector.scalar_tensor_tensor(
                 out=partial[:],
                 in0=xw[:],
                 scalar=-2.0,
-                in1=x2_sb[:, chunks].unsqueeze(2).to_broadcast([P, ROUND_CHUNKS, P]),
+                in1=x2_sb[:, ROUND_CHUNKS * r : ROUND_CHUNKS * (r + 1)]
+                .unsqueeze(2)
+                .to_broadcast([P, ROUND_CHUNKS, P]),
                 op0=ALU.mult,
                 op1=ALU.add,
             )
-            turned = psum.tile([P, ROUND_CHUNKS, P], F32)
+            return partial
+
+        def turn_and_store(r, partial):
+            turned = psum_turn.tile([P, ROUND_CHUNKS, P], F32, tag="turn")
             for c in range(ROUND_CHUNKS):
                 nc.tensor.transpose(turned[:, c, :], partial[:, c, :], ident)
             result = work.tile([P, B, ROUND_ROWS, OUT], F32)
-            nc.scalar.activation(
-                out=result[:].rearrange("o b y z -> o y b z"),
-                in_=turned[:].rearrange("o c (l b z) -> o (c l) b z", l=2, b=B),
-                func=ACT.Relu,
-                bias=w2[:],
-                scale=1.0,
-            )
+            result_v = result[:].rearrange("o b y z -> o y b z")
+            turned_v = turned[:].rearrange("o c (l b z) -> o (c l) b z", l=2, b=B)
+            if r % 2 == 0:
+                nc.scalar.activation(out=result_v, in_=turned_v, func=ACT.Relu, bias=w2[:], scale=1.0)
+            else:
+                nc.vector.tensor_scalar(
+                    out=result_v, in0=turned_v, scalar1=w2[:], scalar2=0.0, op0=ALU.add, op1=ALU.max
+                )
             nc.sync.dma_start(
                 out=out[:, :, ROUND_ROWS * r : ROUND_ROWS * (r + 1), :].rearrange("b o y z -> o b (y z)"),
                 in_=result[:].rearrange("o b y z -> o b (y z)"),
             )
 
+        def patch_sums():
+            x2_ps = psum_small.tile([P, CHUNKS], F32, tag="small")
+            nc.tensor.matmul(
+                out=x2_ps[:], lhsT=taps_same, rhs=pixel_sq[:, 0:CHUNKS], start=True, stop=False
+            )
+            nc.tensor.matmul(
+                out=x2_ps[:], lhsT=taps_next, rhs=pixel_sq[:, 1 : CHUNKS + 1], start=False, stop=True
+            )
+            return x2_ps
+
+        xw = []
+        regroup(0, 0)
+        pixel_sums(0)
         for r in range(ROUNDS):
-            prepare(r)
-            if r > 0:
-                finish(r - 1)
-        nc.vector.quantize_mx(
-            out=x_codes[:, ROUNDS * ROUND_COLS : COLS].bitcast(FP8X4),
-            scales=x_scales[:, ROUNDS * ROUND_COLS : COLS],
-            in_=grouped[:, PACK * ROUNDS * ROUND_COLS : PACK * COLS],
+            if r + 1 < ROUNDS:
+                regroup(r + 1, 0)
+                pixel_sums(r + 1)
+            else:
+                x2_ps = patch_sums()
+            regroup(r, 1)
+            cols = slice(ROUND_COLS * r, ROUND_COLS * (r + 1))
+            quantise(
+                x_codes[:, cols],
+                x_scales[:, cols],
+                grouped[:, PACK * ROUND_COLS * r : PACK * ROUND_COLS * (r + 1)],
+            )
+            if r == 0:
+                quantise(w_codes[:], w_scales[:], w_grouped[:].rearrange("u h o t -> u (h o t)"))
+            else:
+                xw.append(multiply(r - 1))
+        quantise(
+            x_codes[:, ROUNDS * ROUND_COLS : COLS],
+            x_scales[:, ROUNDS * ROUND_COLS : COLS],
+            grouped[:, PACK * ROUNDS * ROUND_COLS : PACK * COLS],
         )
-        finish(ROUNDS - 1)
+        xw.append(multiply(ROUNDS - 1))
+
+        nc.vector.tensor_copy(out=x2_sb[:], in_=x2_ps[:])
+        partials = [combine(r, xw[r]) for r in range(ROUNDS)]
+        for r in range(ROUNDS):
+            turn_and_store(r, partials[r])

@@ -43,7 +43,6 @@ def tile_rbf_conv2d_s_kernel(tc, x, weight, out):
         tc.manual_schedule(),
     ):
         w_sb = keep.tile([P, 1024], BF16)
-        nc.scalar.dma_start(out=w_sb[:], in_=weight)
         raw = []
         for r in range(ROUNDS):
             first, last = image_rows(r)
@@ -56,13 +55,25 @@ def tile_rbf_conv2d_s_kernel(tc, x, weight, out):
                 )
                 raw_r.append(raw_rb)
             raw.append(raw_r)
+            if r == 0:
+                nc.sync.dma_start(out=w_sb[:], in_=weight)
 
-        ident_bf = keep.tile([P, P], BF16)
-        make_identity(nc, ident_bf[:])
         wide = keep.tile([P, 3 * P], F32)
         nc.gpsimd.memset(wide[:], 0.0)
         make_identity(nc, wide[:, P : 2 * P], nomemset=True)
         ident = wide[:, P : 2 * P]
+        ident_bf = keep.tile([P, P], BF16)
+        make_identity(nc, ident_bf[:])
+        pairs = keep.tile([P, 2 * P + ROW], F32)
+        nc.gpsimd.tensor_tensor(
+            out=pairs[:], in0=wide[:, 0 : 2 * P + ROW], in1=wide[:, 1 : 2 * P + ROW + 1], op=ALU.add
+        )
+        taps = keep.tile([P, 2 * P], F32)
+        nc.gpsimd.tensor_tensor(
+            out=taps[:], in0=pairs[:, 0 : 2 * P], in1=pairs[:, ROW : 2 * P + ROW], op=ALU.add
+        )
+        taps_next = taps[:, 0:P]
+        taps_same = taps[:, P : 2 * P]
 
         grouped = keep.tile([P, COLS * PACK], BF16, align_bytes=64)
         grouped_i = grouped[:].bitcast(I32)
@@ -83,30 +94,9 @@ def tile_rbf_conv2d_s_kernel(tc, x, weight, out):
         squares = keep.tile([P, CHUNKS, 2 * P], BF16)
         x2_sb = keep.tile([P, CHUNKS], F32)
 
-        pairs = keep.tile([P, 2 * P + ROW], F32)
-        nc.gpsimd.tensor_tensor(
-            out=pairs[:], in0=wide[:, 0 : 2 * P + ROW], in1=wide[:, 1 : 2 * P + ROW + 1], op=ALU.add
-        )
-        taps = keep.tile([P, 2 * P], F32)
-        nc.gpsimd.tensor_tensor(
-            out=taps[:], in0=pairs[:, 0 : 2 * P], in1=pairs[:, ROW : 2 * P + ROW], op=ALU.add
-        )
-        taps_next = taps[:, 0:P]
-        taps_same = taps[:, P : 2 * P]
-
         w2 = keep.tile([P, 1], F32)
         w_squares = keep.tile([P, 1024], BF16)
-        nc.scalar.activation(out=w_squares[:], in_=w_sb[:], func=ACT.Square, accum_out=w2[:])
-        w_by_k = w_sb[:].rearrange("o (u k) -> o k u", k=8)
-        w_t = psum_small.tile([P, 8, P], BF16, tag="small")
-        for kh in range(2):
-            for kw in range(2):
-                for e in range(2):
-                    nc.tensor.transpose(
-                        w_t[:, 4 * kh + 2 * kw + e, :], w_by_k[:, 4 * e + 2 * kh + kw, :], ident_bf[:]
-                    )
         w_grouped = keep.tile([P, 2, P, PACK], BF16, align_bytes=64)
-        nc.scalar.copy(out=w_grouped[:], in_=w_t[:].rearrange("u (h t) o -> u h o t", h=2))
         w_codes = keep.tile([P, 2 * P], U32, align_bytes=64)
         w_scales = keep.tile([P, 2 * P], U8, align_bytes=64)
 
@@ -120,6 +110,17 @@ def tile_rbf_conv2d_s_kernel(tc, x, weight, out):
                     out=grouped_v[:, first + 1 : last + 1, b, 1 - kw : 1 - kw + SIDE, kw, :],
                     in_=raw[r][b][:].rearrange("p e y z -> p y z e"),
                 )
+
+        def turn_weights():
+            w_by_k = w_sb[:].rearrange("o (u k) -> o k u", k=8)
+            w_t = psum_small.tile([P, 8, P], BF16, tag="small")
+            for kh in range(2):
+                for kw in range(2):
+                    for e in range(2):
+                        nc.tensor.transpose(
+                            w_t[:, 4 * kh + 2 * kw + e, :], w_by_k[:, 4 * e + 2 * kh + kw, :], ident_bf[:]
+                        )
+            nc.scalar.copy(out=w_grouped[:], in_=w_t[:].rearrange("u (h t) o -> u h o t", h=2))
 
         def pixel_sums(r):
             x_t = psum_turn.tile([P, ROUND_CHUNKS, P], F32, tag="turn")
@@ -136,6 +137,16 @@ def tile_rbf_conv2d_s_kernel(tc, x, weight, out):
                     func=ACT.Square,
                     accum_out=pixel_sq[:, chunk : chunk + 1],
                 )
+
+        def patch_sums():
+            x2_ps = psum_small.tile([P, CHUNKS], F32, tag="small")
+            nc.tensor.matmul(
+                out=x2_ps[:], lhsT=taps_same, rhs=pixel_sq[:, 0:CHUNKS], start=True, stop=False
+            )
+            nc.tensor.matmul(
+                out=x2_ps[:], lhsT=taps_next, rhs=pixel_sq[:, 1 : CHUNKS + 1], start=False, stop=True
+            )
+            return x2_ps
 
         def multiply(r):
             xw = psum_xw.tile([P, ROUND_CHUNKS, P], F32)
@@ -185,41 +196,33 @@ def tile_rbf_conv2d_s_kernel(tc, x, weight, out):
                 in_=result[:].rearrange("o b y z -> o b (y z)"),
             )
 
-        def patch_sums():
-            x2_ps = psum_small.tile([P, CHUNKS], F32, tag="small")
-            nc.tensor.matmul(
-                out=x2_ps[:], lhsT=taps_same, rhs=pixel_sq[:, 0:CHUNKS], start=True, stop=False
-            )
-            nc.tensor.matmul(
-                out=x2_ps[:], lhsT=taps_next, rhs=pixel_sq[:, 1 : CHUNKS + 1], start=False, stop=True
-            )
-            return x2_ps
-
         xw = []
         regroup(0, 0)
         pixel_sums(0)
+        turn_weights()
         for r in range(ROUNDS):
+            regroup(r, 1)
             if r + 1 < ROUNDS:
                 regroup(r + 1, 0)
                 pixel_sums(r + 1)
             else:
+                quantise(
+                    x_codes[:, ROUNDS * ROUND_COLS : COLS],
+                    x_scales[:, ROUNDS * ROUND_COLS : COLS],
+                    grouped[:, PACK * ROUNDS * ROUND_COLS : PACK * COLS],
+                )
+                nc.scalar.activation(out=w_squares[:], in_=w_sb[:], func=ACT.Square, accum_out=w2[:])
                 x2_ps = patch_sums()
-            regroup(r, 1)
             cols = slice(ROUND_COLS * r, ROUND_COLS * (r + 1))
             quantise(
                 x_codes[:, cols],
                 x_scales[:, cols],
                 grouped[:, PACK * ROUND_COLS * r : PACK * ROUND_COLS * (r + 1)],
             )
-            if r == 0:
+            if r == 1:
                 quantise(w_codes[:], w_scales[:], w_grouped[:].rearrange("u h o t -> u (h o t)"))
-            else:
+            if r > 0:
                 xw.append(multiply(r - 1))
-        quantise(
-            x_codes[:, ROUNDS * ROUND_COLS : COLS],
-            x_scales[:, ROUNDS * ROUND_COLS : COLS],
-            grouped[:, PACK * ROUNDS * ROUND_COLS : PACK * COLS],
-        )
         xw.append(multiply(ROUNDS - 1))
 
         nc.vector.tensor_copy(out=x2_sb[:], in_=x2_ps[:])

@@ -62,8 +62,6 @@ def tile_rbf_conv2d_s_kernel(tc, x, weight, out):
         nc.gpsimd.memset(wide[:], 0.0)
         make_identity(nc, wide[:, P : 2 * P], nomemset=True)
         ident = wide[:, P : 2 * P]
-        ident_bf = keep.tile([P, P], BF16)
-        make_identity(nc, ident_bf[:])
         pairs = keep.tile([P, 2 * P + ROW], F32)
         nc.gpsimd.tensor_tensor(
             out=pairs[:], in0=wide[:, 0 : 2 * P + ROW], in1=wide[:, 1 : 2 * P + ROW + 1], op=ALU.add
@@ -82,9 +80,7 @@ def tile_rbf_conv2d_s_kernel(tc, x, weight, out):
         nc.vector.memset(grouped_i[:, 2 * COLS - B * row_words : 2 * COLS], 0)
         seams = grouped_i[:, row_words - 1 : 2 * COLS - 1].rearrange("p (s w) -> p s w", w=row_words)
         nc.vector.memset(seams[:, :, 0:2], 0)
-        grouped_v = grouped[:].rearrange(
-            "p (y b z k e) -> p y b z k e", y=PAD_ROWS, b=B, z=OUT, k=2, e=2
-        )
+        grouped_rows = grouped[:].rearrange("p (y b v) -> p y b v", y=PAD_ROWS, b=B)
         grouped_w = grouped[:].bitcast(F32).rearrange("p (c k) -> p c k", k=2)
         x_codes = keep.tile([P, COLS], U32, align_bytes=64)
         x_scales = keep.tile([P, COLS], U8, align_bytes=64)
@@ -96,6 +92,7 @@ def tile_rbf_conv2d_s_kernel(tc, x, weight, out):
 
         w2 = keep.tile([P, 1], F32)
         w_squares = keep.tile([P, 1024], BF16)
+        w_pairs = keep.tile([P, 4, P, 2], BF16)
         w_grouped = keep.tile([P, 2, P, PACK], BF16, align_bytes=64)
         w_codes = keep.tile([P, 2 * P], U32, align_bytes=64)
         w_scales = keep.tile([P, 2 * P], U8, align_bytes=64)
@@ -103,24 +100,32 @@ def tile_rbf_conv2d_s_kernel(tc, x, weight, out):
         def quantise(codes, scales, values):
             nc.vector.quantize_mx(out=codes.bitcast(FP8X4), scales=scales, in_=values)
 
-        def regroup(r, kw):
+        def regroup(r):
             first, last = image_rows(r)
             for b in range(B):
+                pixels = raw[r][b][:].rearrange("p e y u -> p y u e").unsqueeze(3)
                 nc.vector.tensor_copy(
-                    out=grouped_v[:, first + 1 : last + 1, b, 1 - kw : 1 - kw + SIDE, kw, :],
-                    in_=raw[r][b][:].rearrange("p e y z -> p y z e"),
+                    out=grouped_rows[:, first + 1 : last + 1, b, 2 : 2 + 4 * SIDE].rearrange(
+                        "p y (u d e) -> p y u d e", d=2, e=2
+                    ),
+                    in_=pixels.to_broadcast([P, last - first, SIDE, 2, 2]),
                 )
 
+        def sort_weights():
+            nc.scalar.copy(out=w_pairs[:], in_=w_sb[:].rearrange("o (u e j) -> o j u e", e=2, j=4))
+
         def turn_weights():
-            w_by_k = w_sb[:].rearrange("o (u k) -> o k u", k=8)
-            w_t = psum_small.tile([P, 8, P], BF16, tag="small")
-            for kh in range(2):
-                for kw in range(2):
-                    for e in range(2):
-                        nc.tensor.transpose(
-                            w_t[:, 4 * kh + 2 * kw + e, :], w_by_k[:, 4 * e + 2 * kh + kw, :], ident_bf[:]
-                        )
-            nc.scalar.copy(out=w_grouped[:], in_=w_t[:].rearrange("u (h t) o -> u h o t", h=2))
+            w_t = psum_small.tile([P, 4, P], F32, tag="small")
+            for j in range(4):
+                nc.tensor.transpose(
+                    w_t[:, j, :], w_pairs[:, j].rearrange("o u e -> o (u e)").bitcast(F32), ident
+                )
+            nc.scalar.copy(
+                out=w_grouped[:].rearrange("u h o t -> u h (o t)").bitcast(F32).rearrange(
+                    "u h (o k) -> u h o k", k=2
+                ),
+                in_=w_t[:].rearrange("u (h k) o -> u h o k", h=2),
+            )
 
         def pixel_sums(r):
             x_t = psum_turn.tile([P, ROUND_CHUNKS, P], F32, tag="turn")
@@ -197,13 +202,13 @@ def tile_rbf_conv2d_s_kernel(tc, x, weight, out):
             )
 
         xw = []
-        regroup(0, 0)
+        sort_weights()
+        regroup(0)
         pixel_sums(0)
         turn_weights()
         for r in range(ROUNDS):
-            regroup(r, 1)
             if r + 1 < ROUNDS:
-                regroup(r + 1, 0)
+                regroup(r + 1)
                 pixel_sums(r + 1)
             else:
                 quantise(

import concourse.mybir as mybir
from concourse.masks import make_identity

F32 = mybir.dt.float32
BF16 = mybir.dt.bfloat16
I32 = mybir.dt.int32
U32 = mybir.dt.uint32
U8 = mybir.dt.uint8
FP8X4 = mybir.dt.float8_e4m3fn_x4
ACT = mybir.ActivationFunctionType
ALU = mybir.AluOpType

P = 128
PACK = 4
B = 2
SIDE = 31
OUT = 32
PAD_ROWS = OUT + 1
ROW = B * OUT
CHUNK = 128
ROUND_ROWS = 8
ROUND_COLS = ROUND_ROWS * ROW
ROUND_CHUNKS = ROUND_COLS // CHUNK
ROUNDS = OUT // ROUND_ROWS
CHUNKS = ROUNDS * ROUND_CHUNKS
COLS = PAD_ROWS * ROW

FLOPS = 2 * B * OUT * OUT * P * 1024


def image_rows(r):
    return max(ROUND_ROWS * r, 1) - 1, ROUND_ROWS * (r + 1) - 1


def tile_rbf_conv2d_s_kernel(tc, x, weight, out):
    nc = tc.nc
    with (
        tc.tile_pool(name="keep", bufs=1) as keep,
        tc.tile_pool(name="work", bufs=ROUNDS) as work,
        tc.psum_pool(name="psum_small", bufs=1) as psum_small,
        tc.psum_pool(name="psum_turn", bufs=3) as psum_turn,
        tc.psum_pool(name="psum_xw", bufs=ROUNDS) as psum_xw,
        tc.manual_schedule(),
    ):
        w_sb = keep.tile([P, 1024], BF16)
        raw = []
        for r in range(ROUNDS):
            first, last = image_rows(r)
            raw_r = []
            for b in range(B):
                raw_rb = keep.tile([P, 2, last - first, SIDE], BF16, name="raw%d_%d" % (r, b))
                nc.sync.dma_start(
                    out=raw_rb[:].rearrange("p e y z -> p e (y z)"),
                    in_=x[b, :, first:last, :].rearrange("(p e) y z -> p e (y z)", e=2),
                )
                raw_r.append(raw_rb)
            raw.append(raw_r)
            if r == 0:
                nc.sync.dma_start(out=w_sb[:], in_=weight)

        wide = keep.tile([P, 3 * P], F32)
        nc.gpsimd.memset(wide[:], 0.0)
        make_identity(nc, wide[:, P : 2 * P], nomemset=True)
        ident = wide[:, P : 2 * P]
        pairs = keep.tile([P, 2 * P + ROW], F32)
        nc.gpsimd.tensor_tensor(
            out=pairs[:], in0=wide[:, 0 : 2 * P + ROW], in1=wide[:, 1 : 2 * P + ROW + 1], op=ALU.add
        )
        taps = keep.tile([P, 2 * P], F32)
        nc.gpsimd.tensor_tensor(
            out=taps[:], in0=pairs[:, 0 : 2 * P], in1=pairs[:, ROW : 2 * P + ROW], op=ALU.add
        )
        taps_next = taps[:, 0:P]
        taps_same = taps[:, P : 2 * P]

        grouped = keep.tile([P, COLS * PACK], BF16, align_bytes=64)
        grouped_i = grouped[:].bitcast(I32)
        row_words = 2 * OUT
        nc.vector.memset(grouped_i[:, 0 : B * row_words], 0)
        nc.vector.memset(grouped_i[:, 2 * COLS - B * row_words : 2 * COLS], 0)
        seams = grouped_i[:, row_words - 1 : 2 * COLS - 1].rearrange("p (s w) -> p s w", w=row_words)
        nc.vector.memset(seams[:, :, 0:2], 0)
        grouped_rows = grouped[:].rearrange("p (y b v) -> p y b v", y=PAD_ROWS, b=B)
        grouped_w = grouped[:].bitcast(F32).rearrange("p (c k) -> p c k", k=2)
        x_codes = keep.tile([P, COLS], U32, align_bytes=64)
        x_scales = keep.tile([P, COLS], U8, align_bytes=64)

        pixel_sq = keep.tile([P, CHUNKS + 1], F32)
        nc.vector.memset(pixel_sq[:], 0.0)
        squares = keep.tile([P, CHUNKS, 2 * P], BF16)
        x2_sb = keep.tile([P, CHUNKS], F32)

        w2 = keep.tile([P, 1], F32)
        w_squares = keep.tile([P, 1024], BF16)
        w_pairs = keep.tile([P, 4, P, 2], BF16)
        w_grouped = keep.tile([P, 2, P, PACK], BF16, align_bytes=64)
        w_codes = keep.tile([P, 2 * P], U32, align_bytes=64)
        w_scales = keep.tile([P, 2 * P], U8, align_bytes=64)

        def quantise(codes, scales, values):
            nc.vector.quantize_mx(out=codes.bitcast(FP8X4), scales=scales, in_=values)

        def regroup(r):
            first, last = image_rows(r)
            for b in range(B):
                pixels = raw[r][b][:].rearrange("p e y u -> p y u e").unsqueeze(3)
                nc.vector.tensor_copy(
                    out=grouped_rows[:, first + 1 : last + 1, b, 2 : 2 + 4 * SIDE].rearrange(
                        "p y (u d e) -> p y u d e", d=2, e=2
                    ),
                    in_=pixels.to_broadcast([P, last - first, SIDE, 2, 2]),
                )

        def sort_weights():
            nc.scalar.copy(out=w_pairs[:], in_=w_sb[:].rearrange("o (u e j) -> o j u e", e=2, j=4))

        def turn_weights():
            w_t = psum_small.tile([P, 4, P], F32, tag="small")
            for j in range(4):
                nc.tensor.transpose(
                    w_t[:, j, :], w_pairs[:, j].rearrange("o u e -> o (u e)").bitcast(F32), ident
                )
            nc.scalar.copy(
                out=w_grouped[:].rearrange("u h o t -> u h (o t)").bitcast(F32).rearrange(
                    "u h (o k) -> u h o k", k=2
                ),
                in_=w_t[:].rearrange("u (h k) o -> u h o k", h=2),
            )

        def pixel_sums(r):
            x_t = psum_turn.tile([P, ROUND_CHUNKS, P], F32, tag="turn")
            for c in range(ROUND_CHUNKS):
                chunk = ROUND_CHUNKS * r + c
                nc.tensor.transpose(
                    x_t[:, c, :], grouped_w[:, CHUNK * chunk : CHUNK * (chunk + 1), 0], ident
                )
            for c in range(ROUND_CHUNKS):
                chunk = ROUND_CHUNKS * r + c
                nc.scalar.activation(
                    out=squares[:, chunk, :],
                    in_=x_t[:, c, :].bitcast(BF16),
                    func=ACT.Square,
                    accum_out=pixel_sq[:, chunk : chunk + 1],
                )

        def patch_sums():
            x2_ps = psum_small.tile([P, CHUNKS], F32, tag="small")
            nc.tensor.matmul(
                out=x2_ps[:], lhsT=taps_same, rhs=pixel_sq[:, 0:CHUNKS], start=True, stop=False
            )
            nc.tensor.matmul(
                out=x2_ps[:], lhsT=taps_next, rhs=pixel_sq[:, 1 : CHUNKS + 1], start=False, stop=True
            )
            return x2_ps

        def multiply(r):
            xw = psum_xw.tile([P, ROUND_CHUNKS, P], F32)
            for c in range(ROUND_CHUNKS):
                for kh in range(2):
                    start = CHUNK * (ROUND_CHUNKS * r + c) + ROW * kh
                    nc.tensor.matmul_mx(
                        out=xw[:, c, :],
                        lhsT=x_codes[:, start : start + CHUNK].bitcast(FP8X4),
                        lhsT_scale=x_scales[:, start : start + CHUNK],
                        rhs=w_codes[:, P * kh : P * (kh + 1)].bitcast(FP8X4),
                        rhs_scale=w_scales[:, P * kh : P * (kh + 1)],
                        start=(kh == 0),
                        stop=(kh == 1),
                    )
            return xw

        def combine(r, xw):
            partial = work.tile([P, ROUND_CHUNKS, P], F32)
            nc.vector.scalar_tensor_tensor(
                out=partial[:],
                in0=xw[:],
                scalar=-2.0,
                in1=x2_sb[:, ROUND_CHUNKS * r : ROUND_CHUNKS * (r + 1)]
                .unsqueeze(2)
                .to_broadcast([P, ROUND_CHUNKS, P]),
                op0=ALU.mult,
                op1=ALU.add,
            )
            return partial

        def turn_and_store(r, partial):
            turned = psum_turn.tile([P, ROUND_CHUNKS, P], F32, tag="turn")
            for c in range(ROUND_CHUNKS):
                nc.tensor.transpose(turned[:, c, :], partial[:, c, :], ident)
            result = work.tile([P, B, ROUND_ROWS, OUT], F32)
            result_v = result[:].rearrange("o b y z -> o y b z")
            turned_v = turned[:].rearrange("o c (l b z) -> o (c l) b z", l=2, b=B)
            if r % 2 == 0:
                nc.scalar.activation(out=result_v, in_=turned_v, func=ACT.Relu, bias=w2[:], scale=1.0)
            else:
                nc.vector.tensor_scalar(
                    out=result_v, in0=turned_v, scalar1=w2[:], scalar2=0.0, op0=ALU.add, op1=ALU.max
                )
            nc.sync.dma_start(
                out=out[:, :, ROUND_ROWS * r : ROUND_ROWS * (r + 1), :].rearrange("b o y z -> o b (y z)"),
                in_=result[:].rearrange("o b y z -> o b (y z)"),
            )

        xw = []
        sort_weights()
        regroup(0)
        pixel_sums(0)
        turn_weights()
        for r in range(ROUNDS):
            if r + 1 < ROUNDS:
                regroup(r + 1)
                pixel_sums(r + 1)
            else:
                quantise(
                    x_codes[:, ROUNDS * ROUND_COLS : COLS],
                    x_scales[:, ROUNDS * ROUND_COLS : COLS],
                    grouped[:, PACK * ROUNDS * ROUND_COLS : PACK * COLS],
                )
                nc.scalar.activation(out=w_squares[:], in_=w_sb[:], func=ACT.Square, accum_out=w2[:])
                x2_ps = patch_sums()
            cols = slice(ROUND_COLS * r, ROUND_COLS * (r + 1))
            quantise(
                x_codes[:, cols],
                x_scales[:, cols],
                grouped[:, PACK * ROUND_COLS * r : PACK * ROUND_COLS * (r + 1)],
            )
            if r == 1:
                quantise(w_codes[:], w_scales[:], w_grouped[:].rearrange("u h o t -> u (h o t)"))
            if r > 0:
                xw.append(multiply(r - 1))
        xw.append(multiply(ROUNDS - 1))

        nc.vector.tensor_copy(out=x2_sb[:], in_=x2_ps[:])
        partials = [combine(r, xw[r]) for r in range(ROUNDS)]
        for r in range(ROUNDS):
            turn_and_store(r, partials[r])
